import numpy as np
import ml_dtypes


def mxq(x, axis, fmt="e4m3"):
    dtype, down = {"e4m3": (ml_dtypes.float8_e4m3fn, 7), "e5m2": (ml_dtypes.float8_e5m2, 14)}[fmt]
    v = np.moveaxis(np.asarray(x, np.float32).astype(ml_dtypes.bfloat16).astype(np.float64), axis, -1)
    blocks = v.reshape(v.shape[:-1] + (-1, 32))
    amax = np.abs(blocks).max(-1, keepdims=True)
    byte = np.maximum(np.where(amax > 0, np.frexp(amax)[1] - 1 + 127, 0) - down, 1)
    scale = np.exp2(byte - 127.0)
    codes = (blocks / scale).astype(np.float32).astype(dtype).astype(np.float64)
    return np.moveaxis((codes * scale).reshape(v.shape), -1, axis)


WIDE = False


def mx_kscale(k):
    if not WIDE:
        return np.ones(k)
    levels = np.array([10, -10, 5, -5, 0])
    a = np.random.permutation(np.resize(levels, k // 512 * 4)).reshape(k // 512, 4)
    idx = np.arange(k)
    return np.exp2(a[idx // 512, idx % 128 // 32])


BF16 = ml_dtypes.bfloat16


def bf(x):
    return np.asarray(x, np.float32).astype(BF16)


def f64(x):
    return np.asarray(x).astype(np.float64)


E2M1 = np.array([0.0, 0.5, 1.0, 1.5, 2.0, 3.0, 4.0, 6.0, -0.0, -0.5, -1.0, -1.5, -2.0, -3.0, -4.0, -6.0])


def pack_weight(w, fmt):
    k, n = w.shape
    w = f64(bf(w)).reshape(k // 32, 32, n)
    amax = np.abs(w).max(1)
    if fmt == "e4m3":
        byte = np.frexp(amax)[1] - 1 + 127 - 7
    else:
        mant, ex = np.frexp(amax / 6.0)
        byte = np.where(mant > 0.5, ex, ex - 1) + 127
    byte = np.clip(np.where(amax > 0, byte, 1), 1, 254)
    scaled = (w * np.exp2(127.0 - byte)[:, None, :]).reshape(k, n).astype(np.float32)
    by_word = np.ascontiguousarray(scaled.reshape(k // 512, 128, 4, n).transpose(0, 1, 3, 2))
    if fmt == "e4m3":
        words = by_word.astype(ml_dtypes.float8_e4m3fn).view(np.uint8)
    else:
        c = by_word.astype(ml_dtypes.float4_e2m1fn).view(np.uint8) & 0xF
        words = c[..., 0::2] | (c[..., 1::2] << 4)
    return np.ascontiguousarray(words), np.ascontiguousarray(byte.astype(np.uint8).reshape(k // 512, 16, n))


def unpack_weight(words, scales, fmt):
    g, p, n, _ = words.shape
    if fmt == "e4m3":
        vals = np.ascontiguousarray(words).view(ml_dtypes.float8_e4m3fn).astype(np.float64)
    else:
        nib = np.empty((g, p, n, 4), np.uint8)
        nib[..., 0::2] = words & 0xF
        nib[..., 1::2] = words >> 4
        vals = E2M1[nib]
    vals = vals * np.repeat(np.exp2(scales.astype(np.float64) - 127.0), 8, axis=1)[..., None]
    return vals.transpose(0, 1, 3, 2).reshape(g * 512, n)


B, T, G, I, H = 4, 256, 8, 512, 512
FMT = "e4m3"


def setup_inputs():
    s = mx_kscale(I)
    x = bf((np.random.standard_normal((B, T, G, I)) * s).reshape(B, T, G * I))
    w = np.random.standard_normal((G, H, I)) / np.sqrt(I) / s
    stack = np.swapaxes(w, 1, 2)
    words, scales = pack_weight(stack.reshape(-1, H), FMT)
    b = bf(np.random.standard_normal((G, H)) * 0.5)
    return {"x": x, "W_words": words, "W_scales": scales, "b": b}


def reference(x, W_words, W_scales, b):
    xg = f64(x).reshape(B, T, G, I)
    xq = mxq(xg, 3, "e4m3")
    wq = unpack_weight(W_words, W_scales, FMT).reshape(G, I, H)
    y = xq.transpose(2, 0, 1, 3).reshape(G, B * T, I) @ wq
    out = y.reshape(G, B, T, H).transpose(1, 2, 0, 3) + f64(b)
    return np.swapaxes(out, -1, -2).reshape(B, T, G * H)

@@ -1,0 +1,180 @@
+from contextlib import ExitStack
+
+import concourse.mybir as mybir
+from concourse.masks import make_identity
+
+F32 = mybir.dt.float32
+BF16 = mybir.dt.bfloat16
+I32 = mybir.dt.int32
+U32 = mybir.dt.uint32
+U8 = mybir.dt.uint8
+FP8X4 = mybir.dt.float8_e4m3fn_x4
+
+P = 128
+PACK = 4
+TOKENS = 4 * 256
+GROUPS = 8
+FEATURES = 512
+TOKEN_TILES = TOKENS // P
+WORDS = FEATURES // 2
+CHUNK = 128
+CHUNKS = FEATURES // CHUNK
+BANK_GROUPS = 4
+HALVES = GROUPS // BANK_GROUPS
+PAIRS = GROUPS // 2
+CHUNKS_PER_STORE = 2
+
+FLOPS = 2 * TOKENS * GROUPS * FEATURES * FEATURES
+
+assert PAIRS == CHUNKS
+
+
+def tile_groupedlinear_e_kernel(tc, x, W_words, W_scales, b, out):
+    nc = tc.nc
+    x_rows = x.flatten_outer_dims()
+    out_rows = out.flatten_outer_dims()
+
+    with ExitStack() as ctx:
+        ctx.enter_context(tc.manual_schedule())
+        consts = ctx.enter_context(tc.tile_pool(name="consts", bufs=1))
+        x_pool = ctx.enter_context(tc.tile_pool(name="x_pool", bufs=TOKEN_TILES))
+        quant_pool = ctx.enter_context(tc.tile_pool(name="quant_pool", bufs=3))
+        out_pool = ctx.enter_context(tc.tile_pool(name="out_pool", bufs=6))
+        xt_pool = ctx.enter_context(tc.psum_pool(name="xt_pool", bufs=PAIRS))
+        acc_pool = ctx.enter_context(tc.psum_pool(name="acc_pool", bufs=4))
+
+        w_planes = consts.tile([P, GROUPS, FEATURES], U8, align_bytes=64)
+        nc.vector.memset(w_planes[:].bitcast(I32), 0)
+        b_rows = consts.tile([P, FEATURES], BF16)
+        nc.vector.memset(b_rows[:], 0.0)
+        nc.scalar.dma_start(out=b_rows[0:GROUPS, :], in_=b)
+        ident_f32 = consts.tile([P, P], F32)
+        make_identity(nc, ident_f32[:])
+        ident_bf16 = consts.tile([P, P], BF16)
+        nc.vector.tensor_copy(out=ident_bf16[:], in_=ident_f32[:])
+
+        x_tiles = []
+        for i in range(TOKEN_TILES):
+            x_tile = x_pool.tile([P, GROUPS * FEATURES], BF16)
+            x_tiles.append(x_tile)
+        nc.sync.dma_start(out=x_tiles[0][:], in_=x_rows[0:P, :])
+        for quadrant in range(4):
+            nc.sync.dma_start(
+                out=w_planes[32 * quadrant : 32 * quadrant + 4, :, :].bitcast(I32),
+                in_=W_scales[:, 4 * quadrant : 4 * quadrant + 4, :]
+                .rearrange("g r n -> r g n")
+                .bitcast(I32),
+            )
+        w_words = consts.tile([P, GROUPS, FEATURES], U32, align_bytes=64)
+        w_words_dram = W_words.rearrange("g p n t -> p g (n t)").bitcast(I32)
+        for half in range(HALVES):
+            groups = slice(BANK_GROUPS * half, BANK_GROUPS * (half + 1))
+            nc.sync.dma_start(
+                out=w_words[:, groups, :].bitcast(I32), in_=w_words_dram[:, groups, :]
+            )
+        for i in range(1, TOKEN_TILES):
+            nc.sync.dma_start(out=x_tiles[i][:], in_=x_rows[P * i : P * (i + 1), :])
+
+        bias = consts.tile([P, CHUNKS, CHUNK, GROUPS], F32)
+        for c in range(CHUNKS):
+            for half in range(HALVES):
+                acc = acc_pool.tile([P, BANK_GROUPS, CHUNK], F32)
+                for j in range(BANK_GROUPS):
+                    g = BANK_GROUPS * half + j
+                    nc.tensor.matmul(
+                        out=acc[:, j, :],
+                        lhsT=ident_bf16[:, g : g + 1].to_broadcast([P, P]),
+                        rhs=b_rows[:, CHUNK * c : CHUNK * (c + 1)],
+                        start=True,
+                        stop=True,
+                    )
+                copy = nc.vector.tensor_copy if c % 2 == 0 else nc.scalar.copy
+                copy(
+                    out=bias[:, c, :, BANK_GROUPS * half : BANK_GROUPS * (half + 1)],
+                    in_=acc[:].rearrange("p j h -> p h j"),
+                )
+
+        xt_banks = {}
+        grouped = {}
+        x_codes = {}
+        x_planes = {}
+
+        def transpose_tile(i):
+            x_words = x_tiles[i][:].bitcast(F32)
+            for pair in range(PAIRS):
+                xt = xt_pool.tile([P, 2, 2, P], F32)
+                for gg in range(2):
+                    first = WORDS * (2 * pair + gg)
+                    for u in range(2):
+                        nc.tensor.transpose(
+                            out=xt[:, gg, u, :],
+                            in_=x_words[:, first + u : first + WORDS : 2],
+                            identity=ident_f32[:],
+                        )
+                xt_banks[(i, pair)] = xt
+            grouped_tile = quant_pool.tile([P, GROUPS * P * PACK], BF16, align_bytes=64)
+            codes_tile = quant_pool.tile([P, GROUPS * P], U32, align_bytes=64)
+            planes_tile = quant_pool.tile([P, GROUPS * P], U8, align_bytes=64)
+            grouped[i] = grouped_tile
+            x_codes[i] = codes_tile
+            x_planes[i] = planes_tile
+
+        def quantise_pair(i, pair):
+            words = grouped[i][:].bitcast(F32).rearrange(
+                "p (g r u) -> p g r u", g=GROUPS, u=2
+            )
+            nc.scalar.copy(
+                out=words[:, 2 * pair : 2 * pair + 2, :, :],
+                in_=xt_banks[(i, pair)][:].rearrange("p g u r -> p g r u"),
+            )
+            columns = slice(2 * P * pair, 2 * P * (pair + 1))
+            nc.vector.quantize_mx(
+                out=x_codes[i][:, columns].bitcast(FP8X4),
+                scales=x_planes[i][:, columns],
+                in_=grouped[i][:, PACK * 2 * P * pair : PACK * 2 * P * (pair + 1)],
+            )
+
+        def multiply_chunk(i, c, out_chunk):
+            features = slice(CHUNK * c, CHUNK * (c + 1))
+            for half in range(HALVES):
+                acc = acc_pool.tile([P, BANK_GROUPS, CHUNK], F32)
+                for j in range(BANK_GROUPS):
+                    g = BANK_GROUPS * half + j
+                    tokens = slice(P * g, P * (g + 1))
+                    nc.tensor.matmul_mx(
+                        out=acc[:, j, :],
+                        lhsT=x_codes[i][:, tokens].bitcast(FP8X4),
+                        lhsT_scale=x_planes[i][:, tokens],
+                        rhs=w_words[:, g, features].bitcast(FP8X4),
+                        rhs_scale=w_planes[:, g, features],
+                        start=True,
+                        stop=True,
+                    )
+                groups = slice(BANK_GROUPS * half, BANK_GROUPS * (half + 1))
+                nc.vector.tensor_tensor(
+                    out=out_chunk[:, :, groups],
+                    in0=acc[:].rearrange("p j h -> p h j"),
+                    in1=bias[:, c, :, groups],
+                    op=mybir.AluOpType.add,
+                )
+
+        transpose_tile(0)
+        for pair in range(PAIRS):
+            quantise_pair(0, pair)
+        for i in range(TOKEN_TILES):
+            if i + 1 < TOKEN_TILES:
+                transpose_tile(i + 1)
+            for first_chunk in range(0, CHUNKS, CHUNKS_PER_STORE):
+                out_tile = out_pool.tile([P, CHUNKS_PER_STORE, CHUNK, GROUPS], F32)
+                for k in range(CHUNKS_PER_STORE):
+                    c = first_chunk + k
+                    if i + 1 < TOKEN_TILES:
+                        quantise_pair(i + 1, c)
+                    multiply_chunk(i, c, out_tile[:, k, :, :])
+                nc.sync.dma_start(
+                    out=out_rows[
+                        P * i : P * (i + 1),
+                        CHUNK * GROUPS * first_chunk : CHUNK * GROUPS * (first_chunk + CHUNKS_PER_STORE),
+                    ],
+                    in_=out_tile[:].rearrange("p k h g -> p (k h g)"),
+                )

@@ -21,12 +21,9 @@ CHUNK = 128
 CHUNKS = FEATURES // CHUNK
 BANK_GROUPS = 4
 HALVES = GROUPS // BANK_GROUPS
-PAIRS = GROUPS // 2
-CHUNKS_PER_STORE = 2
+CHUNKS_PER_TILE = 2
 
 FLOPS = 2 * TOKENS * GROUPS * FEATURES * FEATURES
-
-assert PAIRS == CHUNKS
 
 
 def tile_groupedlinear_e_kernel(tc, x, W_words, W_scales, b, out):
@@ -38,16 +35,16 @@ def tile_groupedlinear_e_kernel(tc, x, W_words, W_scales, b, out):
         ctx.enter_context(tc.manual_schedule())
         consts = ctx.enter_context(tc.tile_pool(name="consts", bufs=1))
         x_pool = ctx.enter_context(tc.tile_pool(name="x_pool", bufs=TOKEN_TILES))
-        quant_pool = ctx.enter_context(tc.tile_pool(name="quant_pool", bufs=3))
-        out_pool = ctx.enter_context(tc.tile_pool(name="out_pool", bufs=6))
-        xt_pool = ctx.enter_context(tc.psum_pool(name="xt_pool", bufs=PAIRS))
-        acc_pool = ctx.enter_context(tc.psum_pool(name="acc_pool", bufs=4))
+        quant_pool = ctx.enter_context(tc.tile_pool(name="quant_pool", bufs=4))
+        out_pool = ctx.enter_context(tc.tile_pool(name="out_pool", bufs=12))
+        xt_pool = ctx.enter_context(tc.psum_pool(name="xt_pool", bufs=2))
+        acc_pool = ctx.enter_context(tc.psum_pool(name="acc_pool", bufs=6))
 
-        w_planes = consts.tile([P, GROUPS, FEATURES], U8, align_bytes=64)
-        nc.vector.memset(w_planes[:].bitcast(I32), 0)
         b_rows = consts.tile([P, FEATURES], BF16)
         nc.vector.memset(b_rows[:], 0.0)
         nc.scalar.dma_start(out=b_rows[0:GROUPS, :], in_=b)
+        w_planes = consts.tile([P, GROUPS, FEATURES], U8, align_bytes=64)
+        nc.vector.memset(w_planes[:].bitcast(I32), 0)
         ident_f32 = consts.tile([P, P], F32)
         make_identity(nc, ident_f32[:])
         ident_bf16 = consts.tile([P, P], BF16)
@@ -57,7 +54,26 @@ def tile_groupedlinear_e_kernel(tc, x, W_words, W_scales, b, out):
         for i in range(TOKEN_TILES):
             x_tile = x_pool.tile([P, GROUPS * FEATURES], BF16)
             x_tiles.append(x_tile)
-        nc.sync.dma_start(out=x_tiles[0][:], in_=x_rows[0:P, :])
+        w_words = consts.tile([P, GROUPS, FEATURES], U32, align_bytes=64)
+        w_words_dram = W_words.rearrange("g p n t -> p g (n t)").bitcast(I32)
+
+        def load_x(i, first_half, halves):
+            columns = slice(
+                BANK_GROUPS * FEATURES * first_half,
+                BANK_GROUPS * FEATURES * (first_half + halves),
+            )
+            nc.sync.dma_start(
+                out=x_tiles[i][:, columns], in_=x_rows[P * i : P * (i + 1), columns]
+            )
+
+        def load_w(half):
+            groups = slice(BANK_GROUPS * half, BANK_GROUPS * (half + 1))
+            nc.sync.dma_start(
+                out=w_words[:, groups, :].bitcast(I32), in_=w_words_dram[:, groups, :]
+            )
+
+        load_x(0, 0, 1)
+        load_x(1, 0, 1)
         for quadrant in range(4):
             nc.sync.dma_start(
                 out=w_planes[32 * quadrant : 32 * quadrant + 4, :, :].bitcast(I32),
@@ -65,19 +81,17 @@ def tile_groupedlinear_e_kernel(tc, x, W_words, W_scales, b, out):
                 .rearrange("g r n -> r g n")
                 .bitcast(I32),
             )
-        w_words = consts.tile([P, GROUPS, FEATURES], U32, align_bytes=64)
-        w_words_dram = W_words.rearrange("g p n t -> p g (n t)").bitcast(I32)
-        for half in range(HALVES):
-            groups = slice(BANK_GROUPS * half, BANK_GROUPS * (half + 1))
-            nc.sync.dma_start(
-                out=w_words[:, groups, :].bitcast(I32), in_=w_words_dram[:, groups, :]
-            )
-        for i in range(1, TOKEN_TILES):
-            nc.sync.dma_start(out=x_tiles[i][:], in_=x_rows[P * i : P * (i + 1), :])
+        load_w(0)
+        load_x(0, 1, 1)
+        load_w(1)
+        load_x(1, 1, 1)
+        for i in range(2, TOKEN_TILES):
+            load_x(i, 0, HALVES)
 
         bias = consts.tile([P, CHUNKS, CHUNK, GROUPS], F32)
-        for c in range(CHUNKS):
-            for half in range(HALVES):
+
+        def build_bias(half):
+            for c in range(CHUNKS):
                 acc = acc_pool.tile([P, BANK_GROUPS, CHUNK], F32)
                 for j in range(BANK_GROUPS):
                     g = BANK_GROUPS * half + j
@@ -94,87 +108,109 @@ def tile_groupedlinear_e_kernel(tc, x, W_words, W_scales, b, out):
                     in_=acc[:].rearrange("p j h -> p h j"),
                 )
 
-        xt_banks = {}
         grouped = {}
         x_codes = {}
         x_planes = {}
+        out_tiles = {}
 
-        def transpose_tile(i):
+        def transpose_unit(i, half):
             x_words = x_tiles[i][:].bitcast(F32)
-            for pair in range(PAIRS):
+            grouped_tile = quant_pool.tile([P, BANK_GROUPS * P * PACK], BF16, align_bytes=64)
+            codes_tile = quant_pool.tile([P, BANK_GROUPS * P], U32, align_bytes=64)
+            planes_tile = quant_pool.tile([P, BANK_GROUPS * P], U8, align_bytes=64)
+            grouped[(i, half)] = grouped_tile
+            x_codes[(i, half)] = codes_tile
+            x_planes[(i, half)] = planes_tile
+            words = grouped_tile[:].bitcast(F32).rearrange(
+                "p (g r u) -> p g r u", g=BANK_GROUPS, u=2
+            )
+            for pair in range(BANK_GROUPS // 2):
                 xt = xt_pool.tile([P, 2, 2, P], F32)
                 for gg in range(2):
-                    first = WORDS * (2 * pair + gg)
+                    first = WORDS * (BANK_GROUPS * half + 2 * pair + gg)
                     for u in range(2):
                         nc.tensor.transpose(
                             out=xt[:, gg, u, :],
                             in_=x_words[:, first + u : first + WORDS : 2],
                             identity=ident_f32[:],
                         )
-                xt_banks[(i, pair)] = xt
-            grouped_tile = quant_pool.tile([P, GROUPS * P * PACK], BF16, align_bytes=64)
-            codes_tile = quant_pool.tile([P, GROUPS * P], U32, align_bytes=64)
-            planes_tile = quant_pool.tile([P, GROUPS * P], U8, align_bytes=64)
-            grouped[i] = grouped_tile
-            x_codes[i] = codes_tile
-            x_planes[i] = planes_tile
+                nc.scalar.copy(
+                    out=words[:, 2 * pair : 2 * pair + 2, :, :],
+                    in_=xt[:].rearrange("p g u r -> p g r u"),
+                )
 
-        def quantise_pair(i, pair):
-            words = grouped[i][:].bitcast(F32).rearrange(
-                "p (g r u) -> p g r u", g=GROUPS, u=2
-            )
-            nc.scalar.copy(
-                out=words[:, 2 * pair : 2 * pair + 2, :, :],
-                in_=xt_banks[(i, pair)][:].rearrange("p g u r -> p g r u"),
-            )
-            columns = slice(2 * P * pair, 2 * P * (pair + 1))
+        def quantise_unit(i, half):
             nc.vector.quantize_mx(
-                out=x_codes[i][:, columns].bitcast(FP8X4),
-                scales=x_planes[i][:, columns],
-                in_=grouped[i][:, PACK * 2 * P * pair : PACK * 2 * P * (pair + 1)],
+                out=x_codes[(i, half)][:].bitcast(FP8X4),
+                scales=x_planes[(i, half)][:],
+                in_=grouped[(i, half)][:],
             )
 
-        def multiply_chunk(i, c, out_chunk):
+        def multiply_bank(i, half, c):
             features = slice(CHUNK * c, CHUNK * (c + 1))
-            for half in range(HALVES):
-                acc = acc_pool.tile([P, BANK_GROUPS, CHUNK], F32)
-                for j in range(BANK_GROUPS):
-                    g = BANK_GROUPS * half + j
-                    tokens = slice(P * g, P * (g + 1))
-                    nc.tensor.matmul_mx(
-                        out=acc[:, j, :],
-                        lhsT=x_codes[i][:, tokens].bitcast(FP8X4),
-                        lhsT_scale=x_planes[i][:, tokens],
-                        rhs=w_words[:, g, features].bitcast(FP8X4),
-                        rhs_scale=w_planes[:, g, features],
-                        start=True,
-                        stop=True,
-                    )
-                groups = slice(BANK_GROUPS * half, BANK_GROUPS * (half + 1))
-                nc.vector.tensor_tensor(
-                    out=out_chunk[:, :, groups],
-                    in0=acc[:].rearrange("p j h -> p h j"),
-                    in1=bias[:, c, :, groups],
-                    op=mybir.AluOpType.add,
+            acc = acc_pool.tile([P, BANK_GROUPS, CHUNK], F32)
+            for j in range(BANK_GROUPS):
+                g = BANK_GROUPS * half + j
+                tokens = slice(P * j, P * (j + 1))
+                nc.tensor.matmul_mx(
+                    out=acc[:, j, :],
+                    lhsT=x_codes[(i, half)][:, tokens].bitcast(FP8X4),
+                    lhsT_scale=x_planes[(i, half)][:, tokens],
+                    rhs=w_words[:, g, features].bitcast(FP8X4),
+                    rhs_scale=w_planes[:, g, features],
+                    start=True,
+                    stop=True,
                 )
+            key = (i, c // CHUNKS_PER_TILE)
+            if key not in out_tiles:
+                out_tile = out_pool.tile([P, CHUNKS_PER_TILE, CHUNK, GROUPS], F32)
+                out_tiles[key] = out_tile
+            groups = slice(BANK_GROUPS * half, BANK_GROUPS * (half + 1))
+            nc.vector.tensor_tensor(
+                out=out_tiles[key][:, c % CHUNKS_PER_TILE, :, groups],
+                in0=acc[:].rearrange("p j h -> p h j"),
+                in1=bias[:, c, :, groups],
+                op=mybir.AluOpType.add,
+            )
 
-        transpose_tile(0)
-        for pair in range(PAIRS):
-            quantise_pair(0, pair)
-        for i in range(TOKEN_TILES):
-            if i + 1 < TOKEN_TILES:
-                transpose_tile(i + 1)
-            for first_chunk in range(0, CHUNKS, CHUNKS_PER_STORE):
-                out_tile = out_pool.tile([P, CHUNKS_PER_STORE, CHUNK, GROUPS], F32)
-                for k in range(CHUNKS_PER_STORE):
-                    c = first_chunk + k
-                    if i + 1 < TOKEN_TILES:
-                        quantise_pair(i + 1, c)
-                    multiply_chunk(i, c, out_tile[:, k, :, :])
-                nc.sync.dma_start(
-                    out=out_rows[
-                        P * i : P * (i + 1),
-                        CHUNK * GROUPS * first_chunk : CHUNK * GROUPS * (first_chunk + CHUNKS_PER_STORE),
-                    ],
-                    in_=out_tile[:].rearrange("p k h g -> p (k h g)"),
-                )
+        def store(i, first_chunk, chunks):
+            k = first_chunk % CHUNKS_PER_TILE
+            nc.sync.dma_start(
+                out=out_rows[
+                    P * i : P * (i + 1),
+                    CHUNK * GROUPS * first_chunk : CHUNK * GROUPS * (first_chunk + chunks),
+                ],
+                in_=out_tiles[(i, first_chunk // CHUNKS_PER_TILE)][:, k : k + chunks, :, :]
+                .rearrange("p k h g -> p (k h g)"),
+            )
+
+        last = TOKEN_TILES - 1
+        units = [(i, half) for half in range(HALVES) for i in range(2)]
+        units += [(i, half) for i in range(2, TOKEN_TILES) for half in range(HALVES)]
+        steps = []
+        for s in range(len(units) - HALVES):
+            i, half = units[s]
+            prepare = units[s + 1 : s + 2] if s + 1 < len(units) - HALVES else units[s + 1 :]
+            steps.append((prepare, [(i, half, c) for c in range(CHUNKS)]))
+        for first_chunk in range(0, CHUNKS, 2):
+            steps.append(
+                ([], [(last, half, first_chunk + k) for k in range(2) for half in range(HALVES)])
+            )
+
+        build_bias(0)
+        transpose_unit(0, 0)
+        quantise_unit(0, 0)
+        build_bias(1)
+        for prepare, banks in steps:
+            for i, half in prepare:
+                transpose_unit(i, half)
+            for n, (i, half, c) in enumerate(banks):
+                multiply_bank(i, half, c)
+                if n == 1:
+                    for unit in prepare:
+                        quantise_unit(unit[0], unit[1])
+                if half == HALVES - 1:
+                    if i == last:
+                        store(i, c, 1)
+                    elif c % CHUNKS_PER_TILE == CHUNKS_PER_TILE - 1:
+                        store(i, c - (CHUNKS_PER_TILE - 1), CHUNKS_PER_TILE)

@@ -43,7 +43,7 @@ def tile_groupedlinear_e_kernel(tc, x, W_words, W_scales, b, out):
         b_rows = consts.tile([P, FEATURES], BF16)
         nc.vector.memset(b_rows[:], 0.0)
         nc.scalar.dma_start(out=b_rows[0:GROUPS, :], in_=b)
-        w_planes = consts.tile([P, GROUPS, FEATURES], U8, align_bytes=64)
+        w_planes = consts.tile([P, HALVES, FEATURES], U8, align_bytes=64)
         nc.vector.memset(w_planes[:].bitcast(I32), 0)
         ident_f32 = consts.tile([P, P], F32)
         make_identity(nc, ident_f32[:])
@@ -68,19 +68,17 @@ def tile_groupedlinear_e_kernel(tc, x, W_words, W_scales, b, out):
 
         def load_w(half):
             groups = slice(BANK_GROUPS * half, BANK_GROUPS * (half + 1))
+            for quadrant in range(4):
+                nc.sync.dma_start(
+                    out=w_planes[32 * quadrant : 32 * quadrant + 16, half, :].bitcast(I32),
+                    in_=W_scales[groups, 4 * quadrant : 4 * quadrant + 4, :].bitcast(I32),
+                )
             nc.sync.dma_start(
                 out=w_words[:, groups, :].bitcast(I32), in_=w_words_dram[:, groups, :]
             )
 
         load_x(0, 0, 1)
         load_x(1, 0, 1)
-        for quadrant in range(4):
-            nc.sync.dma_start(
-                out=w_planes[32 * quadrant : 32 * quadrant + 4, :, :].bitcast(I32),
-                in_=W_scales[:, 4 * quadrant : 4 * quadrant + 4, :]
-                .rearrange("g r n -> r g n")
-                .bitcast(I32),
-            )
         load_w(0)
         load_x(0, 1, 1)
         load_w(1)
@@ -157,7 +155,7 @@ def tile_groupedlinear_e_kernel(tc, x, W_words, W_scales, b, out):
                     lhsT=x_codes[(i, half)][:, tokens].bitcast(FP8X4),
                     lhsT_scale=x_planes[(i, half)][:, tokens],
                     rhs=w_words[:, g, features].bitcast(FP8X4),
-                    rhs_scale=w_planes[:, g, features],
+                    rhs_scale=w_planes[4 * j : P, half, features],
                     start=True,
                     stop=True,
                 )

@@ -88,7 +88,7 @@ def tile_groupedlinear_e_kernel(tc, x, W_words, W_scales, b, out):
 
         bias = consts.tile([P, CHUNKS, CHUNK, GROUPS], F32)
 
-        def build_bias(half):
+        def build_bias(half, copies):
             for c in range(CHUNKS):
                 acc = acc_pool.tile([P, BANK_GROUPS, CHUNK], F32)
                 for j in range(BANK_GROUPS):
@@ -100,8 +100,7 @@ def tile_groupedlinear_e_kernel(tc, x, W_words, W_scales, b, out):
                         start=True,
                         stop=True,
                     )
-                copy = nc.vector.tensor_copy if c % 2 == 0 else nc.scalar.copy
-                copy(
+                copies[c % len(copies)](
                     out=bias[:, c, :, BANK_GROUPS * half : BANK_GROUPS * (half + 1)],
                     in_=acc[:].rearrange("p j h -> p h j"),
                 )
@@ -195,11 +194,12 @@ def tile_groupedlinear_e_kernel(tc, x, W_words, W_scales, b, out):
                 ([], [(last, half, first_chunk + k) for k in range(2) for half in range(HALVES)])
             )
 
-        build_bias(0)
         transpose_unit(0, 0)
         quantise_unit(0, 0)
-        build_bias(1)
-        for prepare, banks in steps:
+        build_bias(0, [nc.vector.tensor_copy, nc.scalar.copy])
+        for s, (prepare, banks) in enumerate(steps):
+            if s == 1:
+                build_bias(1, [nc.scalar.copy])
             for i, half in prepare:
                 transpose_unit(i, half)
             for n, (i, half, c) in enumerate(banks):

@@ -40,10 +40,10 @@ def tile_groupedlinear_e_kernel(tc, x, W_words, W_scales, b, out):
         xt_pool = ctx.enter_context(tc.psum_pool(name="xt_pool", bufs=2))
         acc_pool = ctx.enter_context(tc.psum_pool(name="acc_pool", bufs=6))
 
-        b_rows = consts.tile([P, FEATURES], BF16)
+        b_rows = consts.tile([P, FEATURES], BF16, align_bytes=256)
         nc.vector.memset(b_rows[:], 0.0)
         nc.scalar.dma_start(out=b_rows[0:GROUPS, :], in_=b)
-        w_planes = consts.tile([P, HALVES, FEATURES], U8, align_bytes=64)
+        w_planes = consts.tile([P, HALVES, FEATURES], U8, align_bytes=256)
         nc.vector.memset(w_planes[:].bitcast(I32), 0)
         ident_f32 = consts.tile([P, P], F32)
         make_identity(nc, ident_f32[:])
@@ -52,9 +52,9 @@ def tile_groupedlinear_e_kernel(tc, x, W_words, W_scales, b, out):
 
         x_tiles = []
         for i in range(TOKEN_TILES):
-            x_tile = x_pool.tile([P, GROUPS * FEATURES], BF16)
+            x_tile = x_pool.tile([P, GROUPS * FEATURES], BF16, align_bytes=256)
             x_tiles.append(x_tile)
-        w_words = consts.tile([P, GROUPS, FEATURES], U32, align_bytes=64)
+        w_words = consts.tile([P, GROUPS, FEATURES], U32, align_bytes=256)
         w_words_dram = W_words.rearrange("g p n t -> p g (n t)").bitcast(I32)
 
         def load_x(i, first_half, halves):
@@ -160,7 +160,7 @@ def tile_groupedlinear_e_kernel(tc, x, W_words, W_scales, b, out):
                 )
             key = (i, c // CHUNKS_PER_TILE)
             if key not in out_tiles:
-                out_tile = out_pool.tile([P, CHUNKS_PER_TILE, CHUNK, GROUPS], F32)
+                out_tile = out_pool.tile([P, CHUNKS_PER_TILE, CHUNK, GROUPS], F32, align_bytes=256)
                 out_tiles[key] = out_tile
             groups = slice(BANK_GROUPS * half, BANK_GROUPS * (half + 1))
             nc.vector.tensor_tensor(

@@ -42,7 +42,6 @@ def tile_groupedlinear_e_kernel(tc, x, W_words, W_scales, b, out):
 
         b_rows = consts.tile([P, FEATURES], BF16, align_bytes=256)
         nc.vector.memset(b_rows[:], 0.0)
-        nc.scalar.dma_start(out=b_rows[0:GROUPS, :], in_=b)
         w_planes = consts.tile([P, HALVES, FEATURES], U8, align_bytes=256)
         nc.vector.memset(w_planes[:].bitcast(I32), 0)
         ident_f32 = consts.tile([P, P], F32)
@@ -79,6 +78,7 @@ def tile_groupedlinear_e_kernel(tc, x, W_words, W_scales, b, out):
 
         load_x(0, 0, 1)
         load_x(1, 0, 1)
+        nc.sync.dma_start(out=b_rows[0:GROUPS, :], in_=b)
         load_w(0)
         load_x(0, 1, 1)
         load_w(1)

@@ -33,13 +33,14 @@ def tile_groupedlinear_e_kernel(tc, x, W_words, W_scales, b, out):
 
     with ExitStack() as ctx:
         ctx.enter_context(tc.manual_schedule())
-        consts = ctx.enter_context(tc.tile_pool(name="consts", bufs=1))
         x_pool = ctx.enter_context(tc.tile_pool(name="x_pool", bufs=TOKEN_TILES))
+        out_pool = ctx.enter_context(tc.tile_pool(name="out_pool", bufs=11))
+        consts = ctx.enter_context(tc.tile_pool(name="consts", bufs=1))
         quant_pool = ctx.enter_context(tc.tile_pool(name="quant_pool", bufs=4))
-        out_pool = ctx.enter_context(tc.tile_pool(name="out_pool", bufs=12))
         xt_pool = ctx.enter_context(tc.psum_pool(name="xt_pool", bufs=2))
         acc_pool = ctx.enter_context(tc.psum_pool(name="acc_pool", bufs=6))
 
+        w_words = consts.tile([P, GROUPS, FEATURES], U32, align_bytes=4096)
         b_rows = consts.tile([P, FEATURES], BF16, align_bytes=256)
         nc.vector.memset(b_rows[:], 0.0)
         w_planes = consts.tile([P, HALVES, FEATURES], U8, align_bytes=256)
@@ -51,9 +52,8 @@ def tile_groupedlinear_e_kernel(tc, x, W_words, W_scales, b, out):
 
         x_tiles = []
         for i in range(TOKEN_TILES):
-            x_tile = x_pool.tile([P, GROUPS * FEATURES], BF16, align_bytes=256)
+            x_tile = x_pool.tile([P, GROUPS * FEATURES], BF16, align_bytes=4096)
             x_tiles.append(x_tile)
-        w_words = consts.tile([P, GROUPS, FEATURES], U32, align_bytes=256)
         w_words_dram = W_words.rearrange("g p n t -> p g (n t)").bitcast(I32)
 
         def load_x(i, first_half, halves):
@@ -160,7 +160,7 @@ def tile_groupedlinear_e_kernel(tc, x, W_words, W_scales, b, out):
                 )
             key = (i, c // CHUNKS_PER_TILE)
             if key not in out_tiles:
-                out_tile = out_pool.tile([P, CHUNKS_PER_TILE, CHUNK, GROUPS], F32, align_bytes=256)
+                out_tile = out_pool.tile([P, CHUNKS_PER_TILE, CHUNK, GROUPS], F32, align_bytes=4096)
                 out_tiles[key] = out_tile
             groups = slice(BANK_GROUPS * half, BANK_GROUPS * (half + 1))
             nc.vector.tensor_tensor(

from contextlib import ExitStack

import concourse.mybir as mybir
from concourse.masks import make_identity

F32 = mybir.dt.float32
BF16 = mybir.dt.bfloat16
I32 = mybir.dt.int32
U32 = mybir.dt.uint32
U8 = mybir.dt.uint8
FP8X4 = mybir.dt.float8_e4m3fn_x4

P = 128
PACK = 4
TOKENS = 4 * 256
GROUPS = 8
FEATURES = 512
TOKEN_TILES = TOKENS // P
WORDS = FEATURES // 2
CHUNK = 128
CHUNKS = FEATURES // CHUNK
BANK_GROUPS = 4
HALVES = GROUPS // BANK_GROUPS
CHUNKS_PER_TILE = 2

FLOPS = 2 * TOKENS * GROUPS * FEATURES * FEATURES


def tile_groupedlinear_e_kernel(tc, x, W_words, W_scales, b, out):
    nc = tc.nc
    x_rows = x.flatten_outer_dims()
    out_rows = out.flatten_outer_dims()

    with ExitStack() as ctx:
        ctx.enter_context(tc.manual_schedule())
        x_pool = ctx.enter_context(tc.tile_pool(name="x_pool", bufs=TOKEN_TILES))
        out_pool = ctx.enter_context(tc.tile_pool(name="out_pool", bufs=11))
        consts = ctx.enter_context(tc.tile_pool(name="consts", bufs=1))
        quant_pool = ctx.enter_context(tc.tile_pool(name="quant_pool", bufs=4))
        xt_pool = ctx.enter_context(tc.psum_pool(name="xt_pool", bufs=2))
        acc_pool = ctx.enter_context(tc.psum_pool(name="acc_pool", bufs=6))

        w_words = consts.tile([P, GROUPS, FEATURES], U32, align_bytes=4096)
        b_rows = consts.tile([P, FEATURES], BF16, align_bytes=256)
        nc.vector.memset(b_rows[:], 0.0)
        w_planes = consts.tile([P, HALVES, FEATURES], U8, align_bytes=256)
        nc.vector.memset(w_planes[:].bitcast(I32), 0)
        ident_f32 = consts.tile([P, P], F32)
        make_identity(nc, ident_f32[:])
        ident_bf16 = consts.tile([P, P], BF16)
        nc.vector.tensor_copy(out=ident_bf16[:], in_=ident_f32[:])

        x_tiles = []
        for i in range(TOKEN_TILES):
            x_tile = x_pool.tile([P, GROUPS * FEATURES], BF16, align_bytes=4096)
            x_tiles.append(x_tile)
        w_words_dram = W_words.rearrange("g p n t -> p g (n t)").bitcast(I32)

        def load_x(i, first_half, halves):
            columns = slice(
                BANK_GROUPS * FEATURES * first_half,
                BANK_GROUPS * FEATURES * (first_half + halves),
            )
            nc.sync.dma_start(
                out=x_tiles[i][:, columns], in_=x_rows[P * i : P * (i + 1), columns]
            )

        def load_w(half):
            groups = slice(BANK_GROUPS * half, BANK_GROUPS * (half + 1))
            for quadrant in range(4):
                nc.sync.dma_start(
                    out=w_planes[32 * quadrant : 32 * quadrant + 16, half, :].bitcast(I32),
                    in_=W_scales[groups, 4 * quadrant : 4 * quadrant + 4, :].bitcast(I32),
                )
            nc.sync.dma_start(
                out=w_words[:, groups, :].bitcast(I32), in_=w_words_dram[:, groups, :]
            )

        load_x(0, 0, 1)
        load_x(1, 0, 1)
        nc.sync.dma_start(out=b_rows[0:GROUPS, :], in_=b)
        load_w(0)
        load_x(0, 1, 1)
        load_w(1)
        load_x(1, 1, 1)
        for i in range(2, TOKEN_TILES):
            load_x(i, 0, HALVES)

        bias = consts.tile([P, CHUNKS, CHUNK, GROUPS], F32)

        def build_bias(half, copies):
            for c in range(CHUNKS):
                acc = acc_pool.tile([P, BANK_GROUPS, CHUNK], F32)
                for j in range(BANK_GROUPS):
                    g = BANK_GROUPS * half + j
                    nc.tensor.matmul(
                        out=acc[:, j, :],
                        lhsT=ident_bf16[:, g : g + 1].to_broadcast([P, P]),
                        rhs=b_rows[:, CHUNK * c : CHUNK * (c + 1)],
                        start=True,
                        stop=True,
                    )
                copies[c % len(copies)](
                    out=bias[:, c, :, BANK_GROUPS * half : BANK_GROUPS * (half + 1)],
                    in_=acc[:].rearrange("p j h -> p h j"),
                )

        grouped = {}
        x_codes = {}
        x_planes = {}
        out_tiles = {}

        def transpose_unit(i, half):
            x_words = x_tiles[i][:].bitcast(F32)
            grouped_tile = quant_pool.tile([P, BANK_GROUPS * P * PACK], BF16, align_bytes=64)
            codes_tile = quant_pool.tile([P, BANK_GROUPS * P], U32, align_bytes=64)
            planes_tile = quant_pool.tile([P, BANK_GROUPS * P], U8, align_bytes=64)
            grouped[(i, half)] = grouped_tile
            x_codes[(i, half)] = codes_tile
            x_planes[(i, half)] = planes_tile
            words = grouped_tile[:].bitcast(F32).rearrange(
                "p (g r u) -> p g r u", g=BANK_GROUPS, u=2
            )
            for pair in range(BANK_GROUPS // 2):
                xt = xt_pool.tile([P, 2, 2, P], F32)
                for gg in range(2):
                    first = WORDS * (BANK_GROUPS * half + 2 * pair + gg)
                    for u in range(2):
                        nc.tensor.transpose(
                            out=xt[:, gg, u, :],
                            in_=x_words[:, first + u : first + WORDS : 2],
                            identity=ident_f32[:],
                        )
                nc.scalar.copy(
                    out=words[:, 2 * pair : 2 * pair + 2, :, :],
                    in_=xt[:].rearrange("p g u r -> p g r u"),
                )

        def quantise_unit(i, half):
            nc.vector.quantize_mx(
                out=x_codes[(i, half)][:].bitcast(FP8X4),
                scales=x_planes[(i, half)][:],
                in_=grouped[(i, half)][:],
            )

        def multiply_bank(i, half, c):
            features = slice(CHUNK * c, CHUNK * (c + 1))
            acc = acc_pool.tile([P, BANK_GROUPS, CHUNK], F32)
            for j in range(BANK_GROUPS):
                g = BANK_GROUPS * half + j
                tokens = slice(P * j, P * (j + 1))
                nc.tensor.matmul_mx(
                    out=acc[:, j, :],
                    lhsT=x_codes[(i, half)][:, tokens].bitcast(FP8X4),
                    lhsT_scale=x_planes[(i, half)][:, tokens],
                    rhs=w_words[:, g, features].bitcast(FP8X4),
                    rhs_scale=w_planes[4 * j : P, half, features],
                    start=True,
                    stop=True,
                )
            key = (i, c // CHUNKS_PER_TILE)
            if key not in out_tiles:
                out_tile = out_pool.tile([P, CHUNKS_PER_TILE, CHUNK, GROUPS], F32, align_bytes=4096)
                out_tiles[key] = out_tile
            groups = slice(BANK_GROUPS * half, BANK_GROUPS * (half + 1))
            nc.vector.tensor_tensor(
                out=out_tiles[key][:, c % CHUNKS_PER_TILE, :, groups],
                in0=acc[:].rearrange("p j h -> p h j"),
                in1=bias[:, c, :, groups],
                op=mybir.AluOpType.add,
            )

        def store(i, first_chunk, chunks):
            k = first_chunk % CHUNKS_PER_TILE
            nc.sync.dma_start(
                out=out_rows[
                    P * i : P * (i + 1),
                    CHUNK * GROUPS * first_chunk : CHUNK * GROUPS * (first_chunk + chunks),
                ],
                in_=out_tiles[(i, first_chunk // CHUNKS_PER_TILE)][:, k : k + chunks, :, :]
                .rearrange("p k h g -> p (k h g)"),
            )

        last = TOKEN_TILES - 1
        units = [(i, half) for half in range(HALVES) for i in range(2)]
        units += [(i, half) for i in range(2, TOKEN_TILES) for half in range(HALVES)]
        steps = []
        for s in range(len(units) - HALVES):
            i, half = units[s]
            prepare = units[s + 1 : s + 2] if s + 1 < len(units) - HALVES else units[s + 1 :]
            steps.append((prepare, [(i, half, c) for c in range(CHUNKS)]))
        for first_chunk in range(0, CHUNKS, 2):
            steps.append(
                ([], [(last, half, first_chunk + k) for k in range(2) for half in range(HALVES)])
            )

        transpose_unit(0, 0)
        quantise_unit(0, 0)
        build_bias(0, [nc.vector.tensor_copy, nc.scalar.copy])
        for s, (prepare, banks) in enumerate(steps):
            if s == 1:
                build_bias(1, [nc.scalar.copy])
            for i, half in prepare:
                transpose_unit(i, half)
            for n, (i, half, c) in enumerate(banks):
                multiply_bank(i, half, c)
                if n == 1:
                    for unit in prepare:
                        quantise_unit(unit[0], unit[1])
                if half == HALVES - 1:
                    if i == last:
                        store(i, c, 1)
                    elif c % CHUNKS_PER_TILE == CHUNKS_PER_TILE - 1:
                        store(i, c - (CHUNKS_PER_TILE - 1), CHUNKS_PER_TILE)
